import numpy as np
import ml_dtypes


def mxq(x, axis, fmt="e4m3"):
    dtype, down = {"e4m3": (ml_dtypes.float8_e4m3fn, 7), "e5m2": (ml_dtypes.float8_e5m2, 14)}[fmt]
    v = np.moveaxis(np.asarray(x, np.float32).astype(ml_dtypes.bfloat16).astype(np.float64), axis, -1)
    blocks = v.reshape(v.shape[:-1] + (-1, 32))
    amax = np.abs(blocks).max(-1, keepdims=True)
    byte = np.maximum(np.where(amax > 0, np.frexp(amax)[1] - 1 + 127, 0) - down, 1)
    scale = np.exp2(byte - 127.0)
    codes = (blocks / scale).astype(np.float32).astype(dtype).astype(np.float64)
    return np.moveaxis((codes * scale).reshape(v.shape), -1, axis)


WIDE = False


def mx_kscale(k):
    if not WIDE:
        return np.ones(k)
    levels = np.array([30, -30])
    if k % 512:
        return np.exp2(np.random.permutation(np.resize(levels, k // 32))).repeat(32)
    a = np.empty((k // 512, 16))
    for p in range(k // 512):
        a[p, :8] = np.random.permutation(np.resize(levels, 8))
        for g in range(8):
            far = levels[np.abs(levels - a[p, g]) >= 10]
            a[p, g + 8] = far[np.random.randint(len(far))]
    return np.exp2(a.ravel()).repeat(32)


BF16 = ml_dtypes.bfloat16


def bf(x):
    return np.asarray(x, np.float32).astype(BF16)


def f64(x):
    return np.asarray(x).astype(np.float64)


E2M1 = np.array([0.0, 0.5, 1.0, 1.5, 2.0, 3.0, 4.0, 6.0, -0.0, -0.5, -1.0, -1.5, -2.0, -3.0, -4.0, -6.0])


def pack_weight(w, fmt):
    k, n = w.shape
    w = f64(bf(w)).reshape(k // 32, 32, n)
    amax = np.abs(w).max(1)
    if fmt == "e4m3":
        byte = np.frexp(amax)[1] - 1 + 127 - 7
    else:
        mant, ex = np.frexp(amax / 6.0)
        byte = np.where(mant > 0.5, ex, ex - 1) + 127
    byte = np.clip(np.where(amax > 0, byte, 1), 1, 254)
    scaled = (w * np.exp2(127.0 - byte)[:, None, :]).reshape(k, n).astype(np.float32)
    by_word = np.ascontiguousarray(scaled.reshape(k // 512, 128, 4, n).transpose(0, 1, 3, 2))
    if fmt == "e4m3":
        words = by_word.astype(ml_dtypes.float8_e4m3fn).view(np.uint8)
    else:
        c = by_word.astype(ml_dtypes.float4_e2m1fn).view(np.uint8) & 0xF
        words = c[..., 0::2] | (c[..., 1::2] << 4)
    return np.ascontiguousarray(words), np.ascontiguousarray(byte.astype(np.uint8).reshape(k // 512, 16, n))


def unpack_weight(words, scales, fmt):
    g, p, n, _ = words.shape
    if fmt == "e4m3":
        vals = np.ascontiguousarray(words).view(ml_dtypes.float8_e4m3fn).astype(np.float64)
    else:
        nib = np.empty((g, p, n, 4), np.uint8)
        nib[..., 0::2] = words & 0xF
        nib[..., 1::2] = words >> 4
        vals = E2M1[nib]
    vals = vals * np.repeat(np.exp2(scales.astype(np.float64) - 127.0), 8, axis=1)[..., None]
    return vals.transpose(0, 1, 3, 2).reshape(g * 512, n)

def pack4(w):
    words, scales = pack_weight(w, "e2m1")
    return words.reshape(words.shape[0], 128, -1), scales


def unpack4(words, scales):
    return unpack_weight(words.reshape(words.shape[0], 128, -1, 2), scales, "e2m1")


B, C, T, E, H = 1, 512, 4, 1024, 8
D = E // H
S = C * T


def heads(y):
    return np.moveaxis(y.reshape(B, C, T, H, D), 3, 1)


def setup_inputs():
    s = mx_kscale(E)
    hidden_states = bf(np.random.standard_normal((B, S, E)) * s)
    wk_words, wk_scales = pack4((np.random.standard_normal((E, E)) * 2.0 / np.sqrt(E) / s[None, :]).T)
    bk = bf(np.random.standard_normal(E) * 0.3)
    wv_words, wv_scales = pack4((np.random.standard_normal((E, E)) * 2.0 / np.sqrt(E) / s[None, :]).T)
    bv = bf(np.random.standard_normal(E) * 0.3)
    return {"hidden_states": hidden_states,
            "wk_words": wk_words,
            "wk_scales": wk_scales,
            "bk": bk,
            "wv_words": wv_words,
            "wv_scales": wv_scales,
            "bv": bv}


def reference(hidden_states, wk_words, wk_scales, bk, wv_words, wv_scales, bv):
    xq = mxq(f64(hidden_states), 2, "e5m2")
    k = heads((xq @ unpack4(wk_words, wk_scales)) + f64(bk))
    v = heads((xq @ unpack4(wv_words, wv_scales)) + f64(bv))
    return k, v, k.mean(axis=3), v.mean(axis=3)

@@ -1,0 +1,217 @@
+from contextlib import ExitStack
+
+import concourse.mybir as mybir
+from concourse.masks import make_identity
+
+F32 = mybir.dt.float32
+BF16 = mybir.dt.bfloat16
+I32 = mybir.dt.int32
+U32 = mybir.dt.uint32
+U8 = mybir.dt.uint8
+E5M2X4 = mybir.dt.float8_e5m2_x4
+E2M1X4 = mybir.dt.float4_e2m1fn_x4
+ADD = mybir.AluOpType.add
+
+P = 128
+E = 1024
+H = 8
+D = 128
+T = 4
+SLOTS = 16
+CHUNKS = SLOTS // T
+PASSES = 2
+BANK = 512
+BANKS = 8
+
+FLOPS = 2 * 2 * (P * SLOTS) * E * E
+
+
+def tile_chunkedattention_pb_kernel(
+    tc, hidden_states, wk_words, wk_scales, bk, wv_words, wv_scales, bv, out_0, out_1, out_2, out_3
+):
+    nc = tc.nc
+    x_hbm = hidden_states[0].rearrange("(p s) e -> p s e", s=SLOTS)
+    y_hbm = [o[0].rearrange("h (p c) t d -> p h (c t d)", c=CHUNKS) for o in (out_0, out_1)]
+    mean_hbm = [o[0].rearrange("h (p c) d -> p h (c d)", c=CHUNKS) for o in (out_2, out_3)]
+    words_hbm = (wk_words, wv_words)
+    scales_hbm = (wk_scales, wv_scales)
+    bias_hbm = (bk, bv)
+
+    with ExitStack() as ctx:
+        keep = ctx.enter_context(tc.tile_pool(name="keep", bufs=1))
+        work = ctx.enter_context(tc.tile_pool(name="work", bufs=2))
+        psum = ctx.enter_context(tc.psum_pool(name="psum", bufs=1))
+        ctx.enter_context(tc.manual_schedule())
+
+        def bank_tile(b, shape):
+            return psum.tile(shape, F32, name="bank%d" % b, tag="bank%d" % b)
+
+        ident = keep.tile([P, P], F32, name="ident")
+        pick = keep.tile([P, 2], BF16, name="pick")
+        bias_rows = keep.tile([P, 2, BANK], BF16, name="bias_rows")
+        bias_all = keep.tile([P, 2, E], F32, name="bias_all")
+        w_words = [keep.tile([P, PASSES, 2 * E], U8, name="w_words%d" % j, align_bytes=64) for j in range(2)]
+        w_scales = [keep.tile([P, PASSES, E], U8, name="w_scales%d" % j, align_bytes=64) for j in range(2)]
+        x_codes = keep.tile([P, SLOTS * PASSES * P], U32, name="x_codes", align_bytes=64)
+        x_scales = keep.tile([P, SLOTS * PASSES * P], U8, name="x_scales", align_bytes=64)
+        means = [keep.tile([P, H, CHUNKS, D], F32, name="means%d" % j) for j in range(2)]
+        x_of_slot = {}
+
+        def load_x(s0, n):
+            x = keep.tile([P, n, E], BF16, name="x%d" % s0)
+            nc.sync.dma_start(out=x[:], in_=x_hbm[:, s0 : s0 + n, :])
+            for i in range(n):
+                x_of_slot[s0 + i] = x[:, i, :]
+
+        def load_scales(j):
+            for q in range(4):
+                nc.sync.dma_start(
+                    out=w_scales[j][32 * q : 32 * q + 4, :, :].bitcast(I32),
+                    in_=scales_hbm[j][:, 4 * q : 4 * q + 4, :].rearrange("g r n -> r g n").bitcast(I32),
+                )
+
+        def load_words(j):
+            nc.sync.dma_start(
+                out=w_words[j][:].bitcast(I32), in_=words_hbm[j].rearrange("g p n -> p g n").bitcast(I32)
+            )
+
+        def load_bias(j):
+            nc.sync.dma_start(out=bias_rows[0:2, j, :], in_=bias_hbm[j].rearrange("(r n) -> r n", r=2))
+
+        def spread_bias(j):
+            for r in range(2):
+                spread = bank_tile(2 * j + r, [P, BANK])
+                nc.tensor.matmul(
+                    spread[:], lhsT=pick[:, r : r + 1].to_broadcast([P, P]), rhs=bias_rows[:, j, :], start=True, stop=True
+                )
+                nc.vector.tensor_copy(out=bias_all[:, j, r * BANK : (r + 1) * BANK], in_=spread[:])
+
+        def transpose_chunk(c):
+            grouped = work.tile([P, T, PASSES, P, 2], F32, name="grouped", align_bytes=64)
+            for i in range(T):
+                pairs = x_of_slot[T * c + i].bitcast(F32)
+                turned = bank_tile(4 + i, [P, PASSES, 2, P])
+                for g in range(PASSES):
+                    for u in range(2):
+                        nc.tensor.transpose(turned[:, g, u, :], pairs[:, 256 * g + u : 256 * (g + 1) : 2], ident[:])
+                nc.scalar.copy(out=grouped[:, i, :, :, :], in_=turned[:].rearrange("p g u r -> p g r u"))
+            return grouped
+
+        def quantize(grouped, c, i0, n):
+            cols = slice((T * c + i0) * PASSES * P, (T * c + i0 + n) * PASSES * P)
+            nc.vector.quantize_mx(
+                out=x_codes[:, cols].bitcast(E5M2X4),
+                scales=x_scales[:, cols],
+                in_=grouped[:, i0 : i0 + n, :, :, :].rearrange("p i g r u -> p (i g r u)").bitcast(BF16),
+            )
+
+        bank_count = [0]
+
+        def project(y, j, h0, heads, s0, slots, banks):
+            width = heads * D
+            per_bank = BANK // width
+            n0 = h0 * D
+            bias = bias_all[:, j, n0 : n0 + width].rearrange("p (h d) -> p h d", d=D)
+            for b0 in range(0, slots, per_bank):
+                acc = bank_tile(bank_count[0] % banks, [P, per_bank, width])
+                bank_count[0] += 1
+                for i in range(per_bank):
+                    for g in range(PASSES):
+                        xc = slice(((s0 + b0 + i) * PASSES + g) * P, ((s0 + b0 + i) * PASSES + g + 1) * P)
+                        nc.tensor.matmul_mx(
+                            out=acc[:, i, :],
+                            lhsT=x_codes[:, xc].bitcast(E5M2X4),
+                            lhsT_scale=x_scales[:, xc],
+                            rhs=w_words[j][:, g, 2 * n0 : 2 * (n0 + width)].bitcast(E2M1X4),
+                            rhs_scale=w_scales[j][:, g, n0 : n0 + width],
+                            start=(g == 0),
+                            stop=(g == PASSES - 1),
+                        )
+                nc.vector.tensor_tensor(
+                    out=y[:, :, b0 : b0 + per_bank, :].rearrange("p h s d -> p s h d"),
+                    in0=acc[:].rearrange("p s (h d) -> p s h d", d=D),
+                    in1=bias.unsqueeze(1).to_broadcast([P, per_bank, heads, D]),
+                    op=ADD,
+                )
+            nc.sync.dma_start(
+                out=y_hbm[j][:, h0 : h0 + heads, s0 * D : (s0 + slots) * D],
+                in_=y[:].rearrange("p h s d -> p h (s d)"),
+            )
+
+        def sum_on_gpsimd(cells, sums, lo, hi):
+            halves = work.tile([P, 6, 2, D], F32, name="halves", bufs=1)
+            nc.gpsimd.tensor_tensor(
+                out=halves[:, lo:hi, :, :], in0=cells[:, lo:hi, 0:2, :], in1=cells[:, lo:hi, 2:4, :], op=ADD
+            )
+            nc.gpsimd.tensor_tensor(
+                out=sums[:, lo:hi, :], in0=halves[:, lo:hi, 0, :], in1=halves[:, lo:hi, 1, :], op=ADD
+            )
+
+        def sum_on_vector(cells, sums, lo, hi):
+            nc.vector.tensor_reduce(
+                out=sums[:, lo:hi, :],
+                in_=cells[:, lo:hi, :, :].rearrange("p m t d -> p m d t"),
+                axis=mybir.AxisListType.X,
+                op=ADD,
+            )
+
+        first_sums = []
+
+        def first_unit(j, h0):
+            y = keep.tile([P, 4, T, D], F32, name="y_first%d_%d" % (j, h0))
+            sums = keep.tile([P, 4, D], F32, name="sums_first%d_%d" % (j, h0))
+            project(y, j, h0, 4, 0, T, 4)
+            sum_on_gpsimd(y, sums, 0, 2)
+            sum_on_gpsimd(y, sums, 2, 4)
+            first_sums.append((j, h0, sums))
+
+        def later_unit(j, h0, on_vector):
+            y = work.tile([P, 2, SLOTS - T, D], F32, name="y_later", bufs=5)
+            sums = work.tile([P, 6, D], F32, name="sums_later", bufs=3)
+            project(y, j, h0, 2, T, SLOTS - T, BANKS)
+            cells = y[:].rearrange("p h (c t) d -> p (h c) t d", t=T)
+            sum_on_vector(cells, sums, 0, on_vector)
+            sum_on_gpsimd(cells, sums, on_vector, 6)
+            nc.scalar.mul(
+                out=means[j][:, h0 : h0 + 2, 1:CHUNKS, :], in_=sums[:].rearrange("p (h c) d -> p h c d", h=2), mul=1.0 / T
+            )
+            nc.scalar.dma_start(
+                out=mean_hbm[j][:, h0 : h0 + 2, :], in_=means[j][:, h0 : h0 + 2, :, :].rearrange("p h c d -> p h (c d)")
+            )
+
+        nc.vector.memset(bias_rows[:].rearrange("p j n -> p (j n)").bitcast(I32), 0)
+        make_identity(nc, ident[:])
+        nc.vector.tensor_copy(out=pick[:], in_=ident[:, 0:2])
+
+        load_x(0, 2)
+        load_x(2, 2)
+        load_scales(0)
+        load_words(0)
+        load_bias(0)
+        load_x(4, 4)
+        load_bias(1)
+        load_scales(1)
+        load_words(1)
+        load_x(8, 4)
+        load_x(12, 4)
+
+        grouped = transpose_chunk(0)
+        spread_bias(0)
+        quantize(grouped, 0, 0, 2)
+        quantize(grouped, 0, 2, 2)
+        spread_bias(1)
+        first_unit(0, 0)
+        first_unit(0, 4)
+        grouped = transpose_chunk(1)
+        first_unit(1, 0)
+        quantize(grouped, 1, 0, T)
+        grouped = transpose_chunk(2)
+        first_unit(1, 4)
+        quantize(grouped, 2, 0, T)
+        grouped = transpose_chunk(3)
+        quantize(grouped, 3, 0, T)
+        for j, h0, sums in first_sums:
+            nc.scalar.mul(out=means[j][:, h0 : h0 + 4, 0, :], in_=sums[:], mul=1.0 / T)
+        for j in range(2):
+            for h0 in range(0, H, 2):
+                later_unit(j, h0, 4 if (j, h0) == (1, H - 2) else 1)

@@ -22,6 +22,7 @@ CHUNKS = SLOTS // T
 PASSES = 2
 BANK = 512
 BANKS = 8
+GSTEP = 2
 
 FLOPS = 2 * 2 * (P * SLOTS) * E * E
 
@@ -47,9 +48,10 @@ def tile_chunkedattention_pb_kernel(
             return psum.tile(shape, F32, name="bank%d" % b, tag="bank%d" % b)
 
         ident = keep.tile([P, P], F32, name="ident")
-        pick = keep.tile([P, 2], BF16, name="pick")
-        bias_rows = keep.tile([P, 2, BANK], BF16, name="bias_rows")
+        pick = keep.tile([P, H], BF16, name="pick")
+        bias_rows = keep.tile([P, 2, D], BF16, name="bias_rows")
         bias_all = keep.tile([P, 2, E], F32, name="bias_all")
+        bias_cols = keep.tile([P, 2, H], F32, name="bias_cols")
         w_words = [keep.tile([P, PASSES, 2 * E], U8, name="w_words%d" % j, align_bytes=64) for j in range(2)]
         w_scales = [keep.tile([P, PASSES, E], U8, name="w_scales%d" % j, align_bytes=64) for j in range(2)]
         x_codes = keep.tile([P, SLOTS * PASSES * P], U32, name="x_codes", align_bytes=64)
@@ -76,36 +78,69 @@ def tile_chunkedattention_pb_kernel(
             )
 
         def load_bias(j):
-            nc.sync.dma_start(out=bias_rows[0:2, j, :], in_=bias_hbm[j].rearrange("(r n) -> r n", r=2))
+            nc.gpsimd.dma_start(out=bias_rows[0:H, j, :], in_=bias_hbm[j].rearrange("(h d) -> h d", d=D))
 
-        def spread_bias(j):
-            for r in range(2):
-                spread = bank_tile(2 * j + r, [P, BANK])
-                nc.tensor.matmul(
-                    spread[:], lhsT=pick[:, r : r + 1].to_broadcast([P, P]), rhs=bias_rows[:, j, :], start=True, stop=True
+        def spread_bias(j, bank0):
+            for half in range(2):
+                spread = bank_tile(bank0 + half, [P, 4, D])
+                for i in range(4):
+                    h = 4 * half + i
+                    nc.tensor.matmul(
+                        spread[:, i, :], lhsT=pick[:, h : h + 1].to_broadcast([P, P]), rhs=bias_rows[:, j, :], start=True, stop=True
+                    )
+                nc.scalar.copy(
+                    out=bias_all[:, j, half * BANK : (half + 1) * BANK], in_=spread[:].rearrange("p i d -> p (i d)")
                 )
-                nc.vector.tensor_copy(out=bias_all[:, j, r * BANK : (r + 1) * BANK], in_=spread[:])
 
-        def transpose_chunk(c):
-            grouped = work.tile([P, T, PASSES, P, 2], F32, name="grouped", align_bytes=64)
-            for i in range(T):
+        def turn_bias():
+            turned = bank_tile(6, [P, 2, H])
+            for j in range(2):
+                nc.tensor.matmul(turned[:, j, :], lhsT=bias_rows[:, j, :], rhs=pick[:], start=True, stop=True)
+            nc.scalar.copy(out=bias_cols[:], in_=turned[:])
+
+        def warm_up(n):
+            idle = keep.tile([P, BANK], BF16, name="idle")
+            nc.vector.memset(idle[:].bitcast(I32), 0)
+            unread = bank_tile(3, [P, BANK])
+            for i in range(n):
+                nc.tensor.matmul(unread[:], lhsT=idle[:, 0:P], rhs=idle[:], start=True, stop=True)
+
+        def sort_chunk(c, copy, n=T):
+            ordered = work.tile([P, T, PASSES, 2, P], F32, name="ordered")
+            for i in range(T - n, T):
                 pairs = x_of_slot[T * c + i].bitcast(F32)
-                turned = bank_tile(4 + i, [P, PASSES, 2, P])
-                for g in range(PASSES):
+                copy(out=ordered[:, i, :, :, :], in_=pairs.rearrange("p (g r u) -> p g u r", g=PASSES, u=2))
+            return ordered
+
+        def transpose_chunk(c, order):
+            grouped = work.tile([P, PASSES, T, P, 2], F32, name="grouped", align_bytes=64)
+            for b, (g, a) in enumerate(order):
+                turned = bank_tile(4 + b, [P, 2, 2, P])
+                for i in range(2):
+                    pairs = x_of_slot[T * c + a + i].bitcast(F32)
                     for u in range(2):
-                        nc.tensor.transpose(turned[:, g, u, :], pairs[:, 256 * g + u : 256 * (g + 1) : 2], ident[:])
-                nc.scalar.copy(out=grouped[:, i, :, :, :], in_=turned[:].rearrange("p g u r -> p g r u"))
+                        nc.tensor.transpose(turned[:, i, u, :], pairs[:, 256 * g + u : 256 * (g + 1) : 2], ident[:])
+                nc.scalar.copy(out=grouped[:, g, a : a + 2, :, :], in_=turned[:].rearrange("p i u r -> p i r u"))
             return grouped
 
-        def quantize(grouped, c, i0, n):
-            cols = slice((T * c + i0) * PASSES * P, (T * c + i0 + n) * PASSES * P)
+        def x_cols(c, g, i, n):
+            first = ((c * PASSES + g) * T + i) * P
+            return slice(first, first + n * P)
+
+        def quantize(grouped, c, g, i, n):
+            values = grouped[:].rearrange("p g i r u -> p (g i r u)")
+            first = (g * T + i) * P * 2
             nc.vector.quantize_mx(
-                out=x_codes[:, cols].bitcast(E5M2X4),
-                scales=x_scales[:, cols],
-                in_=grouped[:, i0 : i0 + n, :, :, :].rearrange("p i g r u -> p (i g r u)").bitcast(BF16),
+                out=x_codes[:, x_cols(c, g, i, n)].bitcast(E5M2X4),
+                scales=x_scales[:, x_cols(c, g, i, n)],
+                in_=values[:, first : first + n * P * 2].bitcast(BF16),
             )
 
         bank_count = [0]
+
+        def next_bank(banks, shape):
+            bank_count[0] += 1
+            return bank_tile((bank_count[0] - 1) % banks, shape)
 
         def project(y, j, h0, heads, s0, slots, banks):
             width = heads * D
@@ -113,11 +148,10 @@ def tile_chunkedattention_pb_kernel(
             n0 = h0 * D
             bias = bias_all[:, j, n0 : n0 + width].rearrange("p (h d) -> p h d", d=D)
             for b0 in range(0, slots, per_bank):
-                acc = bank_tile(bank_count[0] % banks, [P, per_bank, width])
-                bank_count[0] += 1
+                acc = next_bank(banks, [P, per_bank, width])
                 for i in range(per_bank):
                     for g in range(PASSES):
-                        xc = slice(((s0 + b0 + i) * PASSES + g) * P, ((s0 + b0 + i) * PASSES + g + 1) * P)
+                        xc = x_cols((s0 + b0 + i) // T, g, (s0 + b0 + i) % T, 1)
                         nc.tensor.matmul_mx(
                             out=acc[:, i, :],
                             lhsT=x_codes[:, xc].bitcast(E5M2X4),
@@ -133,85 +167,143 @@ def tile_chunkedattention_pb_kernel(
                     in1=bias.unsqueeze(1).to_broadcast([P, per_bank, heads, D]),
                     op=ADD,
                 )
+
+        def project_turned(j, h, c):
+            acc = next_bank(BANKS, [P, BANK])
+            for g in range(PASSES):
+                nc.tensor.matmul_mx(
+                    out=acc[:],
+                    lhsT=w_words[j][:, g, 2 * h * D : 2 * (h + 1) * D].bitcast(E2M1X4),
+                    lhsT_scale=w_scales[j][:, g, h * D : (h + 1) * D],
+                    rhs=x_codes[:, x_cols(c, g, 0, T)].bitcast(E5M2X4),
+                    rhs_scale=x_scales[:, x_cols(c, g, 0, T)],
+                    start=(g == 0),
+                    stop=(g == PASSES - 1),
+                )
+            y_turned = work.tile([P, T, P], F32, name="y_turned", bufs=2)
+            nc.scalar.activation(
+                out=y_turned[:].rearrange("p i r -> p (i r)"),
+                in_=acc[:],
+                func=mybir.ActivationFunctionType.Identity,
+                bias=bias_cols[:, j, h : h + 1],
+            )
+            return y_turned
+
+        def turn_back(y_turned, y_cell):
+            back = next_bank(BANKS, [P, T, D])
+            for i in range(T):
+                nc.tensor.transpose(back[:, i, :], y_turned[:, i, :], ident[:])
+            nc.scalar.copy(out=y_cell, in_=back[:])
+
+        def store(y, j, h0, heads, s0, a, b):
             nc.sync.dma_start(
-                out=y_hbm[j][:, h0 : h0 + heads, s0 * D : (s0 + slots) * D],
-                in_=y[:].rearrange("p h s d -> p h (s d)"),
+                out=y_hbm[j][:, h0 : h0 + heads, (s0 + a) * D : (s0 + b) * D],
+                in_=y[:, :, a:b, :].rearrange("p h s d -> p h (s d)"),
             )
 
-        def sum_on_gpsimd(cells, sums, lo, hi):
-            halves = work.tile([P, 6, 2, D], F32, name="halves", bufs=1)
-            nc.gpsimd.tensor_tensor(
-                out=halves[:, lo:hi, :, :], in0=cells[:, lo:hi, 0:2, :], in1=cells[:, lo:hi, 2:4, :], op=ADD
-            )
-            nc.gpsimd.tensor_tensor(
-                out=sums[:, lo:hi, :], in0=halves[:, lo:hi, 0, :], in1=halves[:, lo:hi, 1, :], op=ADD
-            )
+        def sum_on_gpsimd(cells, sums):
+            a, b = cells.shape[1], cells.shape[2]
+            halves = work.tile([P, a, b, 2 * D], F32, name="halves", bufs=1)
+            nc.gpsimd.tensor_tensor(out=halves[:], in0=cells[:, :, :, 0 : 2 * D], in1=cells[:, :, :, 2 * D : 4 * D], op=ADD)
+            nc.gpsimd.tensor_tensor(out=sums, in0=halves[:, :, :, 0:D], in1=halves[:, :, :, D : 2 * D], op=ADD)
 
-        def sum_on_vector(cells, sums, lo, hi):
+        def sum_on_vector(cells, sums):
             nc.vector.tensor_reduce(
-                out=sums[:, lo:hi, :],
-                in_=cells[:, lo:hi, :, :].rearrange("p m t d -> p m d t"),
-                axis=mybir.AxisListType.X,
-                op=ADD,
+                out=sums, in_=cells.rearrange("p m (t d) -> p m d t", t=T), axis=mybir.AxisListType.X, op=ADD
             )
 
-        first_sums = []
+        def finish_means(j, h0):
+            part = means[j][:, h0 : h0 + 2, :, :].rearrange("p h c d -> p h (c d)")
+            nc.scalar.mul(out=part, in_=part, mul=1.0 / T)
+            nc.scalar.dma_start(out=mean_hbm[j][:, h0 : h0 + 2, :], in_=part)
 
-        def first_unit(j, h0):
-            y = keep.tile([P, 4, T, D], F32, name="y_first%d_%d" % (j, h0))
-            sums = keep.tile([P, 4, D], F32, name="sums_first%d_%d" % (j, h0))
-            project(y, j, h0, 4, 0, T, 4)
-            sum_on_gpsimd(y, sums, 0, 2)
-            sum_on_gpsimd(y, sums, 2, 4)
-            first_sums.append((j, h0, sums))
+        def wide_unit(j, h0, c, on_vector):
+            y = keep.tile([P, 4, T, D], F32, name="y_wide%d_%d_%d" % (j, h0, c))
+            project(y, j, h0, 4, T * c, T, 4)
+            store(y, j, h0, 4, T * c, 0, T)
+            cells = y[:].rearrange("p h (c t) d -> p h c (t d)", t=T)
+            if on_vector:
+                sum_on_vector(cells[:, 0:on_vector, 0, :], means[j][:, h0 : h0 + on_vector, c, :])
+            for a in range(on_vector, 4, GSTEP):
+                b = min(4, a + GSTEP)
+                if b > a:
+                    sum_on_gpsimd(cells[:, a:b, :, :], means[j][:, h0 + a : h0 + b, c : c + 1, :])
 
-        def later_unit(j, h0, on_vector):
-            y = work.tile([P, 2, SLOTS - T, D], F32, name="y_later", bufs=5)
-            sums = work.tile([P, 6, D], F32, name="sums_later", bufs=3)
-            project(y, j, h0, 2, T, SLOTS - T, BANKS)
-            cells = y[:].rearrange("p h (c t) d -> p (h c) t d", t=T)
-            sum_on_vector(cells, sums, 0, on_vector)
-            sum_on_gpsimd(cells, sums, on_vector, 6)
-            nc.scalar.mul(
-                out=means[j][:, h0 : h0 + 2, 1:CHUNKS, :], in_=sums[:].rearrange("p (h c) d -> p h c d", h=2), mul=1.0 / T
-            )
-            nc.scalar.dma_start(
-                out=mean_hbm[j][:, h0 : h0 + 2, :], in_=means[j][:, h0 : h0 + 2, :, :].rearrange("p h c d -> p h (c d)")
-            )
+        def long_unit(j, h0, c0, turn, on_vector, split):
+            n = CHUNKS - c0
+            y = work.tile([P, 2, n * T, D], F32, name="y_long", bufs=4)
+            cells = y[:].rearrange("p h (c t) d -> p h c (t d)", t=T)
+            sums = means[j][:, h0 : h0 + 2, c0:CHUNKS, :]
+            if turn:
+                turned = [project_turned(j, h0 + i, c0) for i in range(2)]
+                project(y[:, :, T : n * T, :], j, h0, 2, (c0 + 1) * T, (n - 1) * T, BANKS)
+                for i in range(2):
+                    turn_back(turned[i], y[:, i, 0:T, :])
+                store(y, j, h0, 2, c0 * T, 0, n * T)
+            elif split:
+                project(y, j, h0, 2, c0 * T, (n - 1) * T, BANKS)
+                store(y, j, h0, 2, c0 * T, 0, (n - 1) * T)
+                project(y[:, :, (n - 1) * T : n * T, :], j, h0, 2, (CHUNKS - 1) * T, T, BANKS)
+                store(y, j, h0, 2, c0 * T, (n - 1) * T, n * T)
+            else:
+                project(y, j, h0, 2, c0 * T, n * T, BANKS)
+                store(y, j, h0, 2, c0 * T, 0, n * T)
+            for c in range(n - on_vector, n):
+                sum_on_vector(cells[:, :, c, :], sums[:, :, c, :])
+            if n > on_vector:
+                sum_on_gpsimd(cells[:, :, 0 : n - on_vector, :], sums[:, :, 0 : n - on_vector, :])
 
-        nc.vector.memset(bias_rows[:].rearrange("p j n -> p (j n)").bitcast(I32), 0)
+        nc.gpsimd.memset(bias_rows[:].rearrange("p j n -> p (j n)").bitcast(I32), 0)
         make_identity(nc, ident[:])
-        nc.vector.tensor_copy(out=pick[:], in_=ident[:, 0:2])
+        nc.scalar.activation(out=pick[:], in_=ident[:, 0:H], func=mybir.ActivationFunctionType.Identity)
 
+        load_bias(0)
+        load_bias(1)
         load_x(0, 2)
         load_x(2, 2)
         load_scales(0)
         load_words(0)
-        load_bias(0)
         load_x(4, 4)
-        load_bias(1)
         load_scales(1)
         load_words(1)
         load_x(8, 4)
         load_x(12, 4)
 
-        grouped = transpose_chunk(0)
-        spread_bias(0)
-        quantize(grouped, 0, 0, 2)
-        quantize(grouped, 0, 2, 2)
-        spread_bias(1)
-        first_unit(0, 0)
-        first_unit(0, 4)
-        grouped = transpose_chunk(1)
-        first_unit(1, 0)
-        quantize(grouped, 1, 0, T)
-        grouped = transpose_chunk(2)
-        first_unit(1, 4)
-        quantize(grouped, 2, 0, T)
-        grouped = transpose_chunk(3)
-        quantize(grouped, 3, 0, T)
-        for j, h0, sums in first_sums:
-            nc.scalar.mul(out=means[j][:, h0 : h0 + 4, 0, :], in_=sums[:], mul=1.0 / T)
-        for j in range(2):
-            for h0 in range(0, H, 2):
-                later_unit(j, h0, 4 if (j, h0) == (1, H - 2) else 1)
+        grouped = {}
+        ordered = {}
+        grouped[0] = transpose_chunk(0, [(0, 0), (1, 0), (0, 2), (1, 2)])
+        spread_bias(0, 4)
+        for i in (0, 2):
+            for g in range(PASSES):
+                quantize(grouped[0], 0, g, i, 2)
+        wide_unit(0, 0, 0, 0)
+        spread_bias(1, 4)
+        turn_bias()
+        wide_unit(0, 4, 0, 0)
+        grouped[1] = transpose_chunk(1, [(0, 0), (0, 2), (1, 0), (1, 2)])
+        wide_unit(1, 0, 0, 0)
+        quantize(grouped[1], 1, 0, 0, T)
+        quantize(grouped[1], 1, 1, 0, T)
+        grouped[2] = transpose_chunk(2, [(0, 0), (0, 2), (1, 0), (1, 2)])
+        wide_unit(1, 4, 0, 0)
+        quantize(grouped[2], 2, 0, 0, T)
+        quantize(grouped[2], 2, 1, 0, T)
+        grouped[3] = transpose_chunk(3, [(0, 0), (0, 2), (1, 0), (1, 2)])
+        quantize(grouped[3], 3, 0, 0, T)
+        quantize(grouped[3], 3, 1, 0, T)
+        long_unit(0, 0, 1, 0, 0, 0)
+        long_unit(0, 2, 1, 1, 1, 0)
+        long_unit(0, 4, 1, 1, 1, 0)
+        finish_means(0, 0)
+        long_unit(0, 6, 1, 1, 1, 0)
+        finish_means(0, 2)
+        long_unit(1, 0, 1, 1, 1, 0)
+        finish_means(0, 4)
+        long_unit(1, 2, 1, 1, 1, 0)
+        finish_means(0, 6)
+        long_unit(1, 4, 1, 1, 2, 0)
+        finish_means(1, 0)
+        finish_means(1, 2)
+        long_unit(1, 6, 1, 0, 2, 1)
+        finish_means(1, 4)
+        finish_means(1, 6)

@@ -52,24 +52,24 @@ def tile_chunkedattention_pb_kernel(
         bias_rows = keep.tile([P, 2, D], BF16, name="bias_rows")
         bias_all = keep.tile([P, 2, E], F32, name="bias_all")
         bias_cols = keep.tile([P, 2, H], F32, name="bias_cols")
-        w_words = [keep.tile([P, PASSES, 2 * E], U8, name="w_words%d" % j, align_bytes=64) for j in range(2)]
-        w_scales = [keep.tile([P, PASSES, E], U8, name="w_scales%d" % j, align_bytes=64) for j in range(2)]
-        x_codes = keep.tile([P, SLOTS * PASSES * P], U32, name="x_codes", align_bytes=64)
-        x_scales = keep.tile([P, SLOTS * PASSES * P], U8, name="x_scales", align_bytes=64)
-        means = [keep.tile([P, H, CHUNKS, D], F32, name="means%d" % j) for j in range(2)]
+        w_words = [keep.tile([P, PASSES, 2 * E], U8, name="w_words%d" % j, align_bytes=256) for j in range(2)]
+        w_scales = [keep.tile([P, PASSES, E], U8, name="w_scales%d" % j, align_bytes=256) for j in range(2)]
+        x_codes = keep.tile([P, SLOTS * PASSES * P], U32, name="x_codes", align_bytes=256)
+        x_scales = keep.tile([P, SLOTS * PASSES * P], U8, name="x_scales", align_bytes=256)
+        means = [keep.tile([P, H, CHUNKS, D], F32, name="means%d" % j, align_bytes=256) for j in range(2)]
         x_of_slot = {}
 
         def load_x(s0, n):
-            x = keep.tile([P, n, E], BF16, name="x%d" % s0)
+            x = keep.tile([P, n, E], BF16, name="x%d" % s0, align_bytes=256)
             nc.sync.dma_start(out=x[:], in_=x_hbm[:, s0 : s0 + n, :])
             for i in range(n):
                 x_of_slot[s0 + i] = x[:, i, :]
 
         def load_scales(j):
-            for q in range(4):
+            for r in range(4):
                 nc.sync.dma_start(
-                    out=w_scales[j][32 * q : 32 * q + 4, :, :].bitcast(I32),
-                    in_=scales_hbm[j][:, 4 * q : 4 * q + 4, :].rearrange("g r n -> r g n").bitcast(I32),
+                    out=w_scales[j][r:P:32, :, :].bitcast(I32),
+                    in_=scales_hbm[j][:, r:16:4, :].rearrange("g q n -> q g n").bitcast(I32),
                 )
 
         def load_words(j):
@@ -113,7 +113,7 @@ def tile_chunkedattention_pb_kernel(
             return ordered
 
         def transpose_chunk(c, order):
-            grouped = work.tile([P, PASSES, T, P, 2], F32, name="grouped", align_bytes=64)
+            grouped = work.tile([P, PASSES, T, P, 2], F32, name="grouped", align_bytes=256)
             for b, (g, a) in enumerate(order):
                 turned = bank_tile(4 + b, [P, 2, 2, P])
                 for i in range(2):
@@ -218,7 +218,7 @@ def tile_chunkedattention_pb_kernel(
             nc.scalar.dma_start(out=mean_hbm[j][:, h0 : h0 + 2, :], in_=part)
 
         def wide_unit(j, h0, c, on_vector):
-            y = keep.tile([P, 4, T, D], F32, name="y_wide%d_%d_%d" % (j, h0, c))
+            y = keep.tile([P, 4, T, D], F32, name="y_wide%d_%d_%d" % (j, h0, c), align_bytes=256)
             project(y, j, h0, 4, T * c, T, 4)
             store(y, j, h0, 4, T * c, 0, T)
             cells = y[:].rearrange("p h (c t) d -> p h c (t d)", t=T)
@@ -231,7 +231,7 @@ def tile_chunkedattention_pb_kernel(
 
         def long_unit(j, h0, c0, turn, on_vector, split):
             n = CHUNKS - c0
-            y = work.tile([P, 2, n * T, D], F32, name="y_long", bufs=4)
+            y = work.tile([P, 2, n * T, D], F32, name="y_long", bufs=4, align_bytes=256)
             cells = y[:].rearrange("p h (c t) d -> p h c (t d)", t=T)
             sums = means[j][:, h0 : h0 + 2, c0:CHUNKS, :]
             if turn:
@@ -291,7 +291,7 @@ def tile_chunkedattention_pb_kernel(
         grouped[3] = transpose_chunk(3, [(0, 0), (0, 2), (1, 0), (1, 2)])
         quantize(grouped[3], 3, 0, 0, T)
         quantize(grouped[3], 3, 1, 0, T)
-        long_unit(0, 0, 1, 0, 0, 0)
+        long_unit(0, 0, 1, 0, 0, 1)
         long_unit(0, 2, 1, 1, 1, 0)
         long_unit(0, 4, 1, 1, 1, 0)
         finish_means(0, 0)

@@ -229,6 +229,18 @@ def tile_chunkedattention_pb_kernel(
                 if b > a:
                     sum_on_gpsimd(cells[:, a:b, :, :], means[j][:, h0 + a : h0 + b, c : c + 1, :])
 
+        def part_unit(j, h0, c0, c1, on_vector):
+            n = c1 - c0
+            y = keep.tile([P, 2, n * T, D], F32, name="y_part%d_%d_%d" % (j, h0, c0))
+            cells = y[:].rearrange("p h (c t) d -> p h c (t d)", t=T)
+            sums = means[j][:, h0 : h0 + 2, c0:c1, :]
+            project(y, j, h0, 2, c0 * T, n * T, 4)
+            store(y, j, h0, 2, c0 * T, 0, n * T)
+            for c in range(n - on_vector, n):
+                sum_on_vector(cells[:, :, c, :], sums[:, :, c, :])
+            for c in range(n - on_vector):
+                sum_on_gpsimd(cells[:, :, c : c + 1, :], sums[:, :, c : c + 1, :])
+
         def long_unit(j, h0, c0, turn, on_vector, split):
             n = CHUNKS - c0
             y = work.tile([P, 2, n * T, D], F32, name="y_long", bufs=4, align_bytes=256)
@@ -268,7 +280,7 @@ def tile_chunkedattention_pb_kernel(
         load_words(1)
         load_x(8, 4)
         load_x(12, 4)
-
+        warm_up(6)
         grouped = {}
         ordered = {}
         grouped[0] = transpose_chunk(0, [(0, 0), (1, 0), (0, 2), (1, 2)])

from contextlib import ExitStack

import concourse.mybir as mybir
from concourse.masks import make_identity

F32 = mybir.dt.float32
BF16 = mybir.dt.bfloat16
I32 = mybir.dt.int32
U32 = mybir.dt.uint32
U8 = mybir.dt.uint8
E5M2X4 = mybir.dt.float8_e5m2_x4
E2M1X4 = mybir.dt.float4_e2m1fn_x4
ADD = mybir.AluOpType.add

P = 128
E = 1024
H = 8
D = 128
T = 4
SLOTS = 16
CHUNKS = SLOTS // T
PASSES = 2
BANK = 512
BANKS = 8
GSTEP = 2

FLOPS = 2 * 2 * (P * SLOTS) * E * E


def tile_chunkedattention_pb_kernel(
    tc, hidden_states, wk_words, wk_scales, bk, wv_words, wv_scales, bv, out_0, out_1, out_2, out_3
):
    nc = tc.nc
    x_hbm = hidden_states[0].rearrange("(p s) e -> p s e", s=SLOTS)
    y_hbm = [o[0].rearrange("h (p c) t d -> p h (c t d)", c=CHUNKS) for o in (out_0, out_1)]
    mean_hbm = [o[0].rearrange("h (p c) d -> p h (c d)", c=CHUNKS) for o in (out_2, out_3)]
    words_hbm = (wk_words, wv_words)
    scales_hbm = (wk_scales, wv_scales)
    bias_hbm = (bk, bv)

    with ExitStack() as ctx:
        keep = ctx.enter_context(tc.tile_pool(name="keep", bufs=1))
        work = ctx.enter_context(tc.tile_pool(name="work", bufs=2))
        psum = ctx.enter_context(tc.psum_pool(name="psum", bufs=1))
        ctx.enter_context(tc.manual_schedule())

        def bank_tile(b, shape):
            return psum.tile(shape, F32, name="bank%d" % b, tag="bank%d" % b)

        ident = keep.tile([P, P], F32, name="ident")
        pick = keep.tile([P, H], BF16, name="pick")
        bias_rows = keep.tile([P, 2, D], BF16, name="bias_rows")
        bias_all = keep.tile([P, 2, E], F32, name="bias_all")
        bias_cols = keep.tile([P, 2, H], F32, name="bias_cols")
        w_words = [keep.tile([P, PASSES, 2 * E], U8, name="w_words%d" % j, align_bytes=256) for j in range(2)]
        w_scales = [keep.tile([P, PASSES, E], U8, name="w_scales%d" % j, align_bytes=256) for j in range(2)]
        x_codes = keep.tile([P, SLOTS * PASSES * P], U32, name="x_codes", align_bytes=256)
        x_scales = keep.tile([P, SLOTS * PASSES * P], U8, name="x_scales", align_bytes=256)
        means = [keep.tile([P, H, CHUNKS, D], F32, name="means%d" % j, align_bytes=256) for j in range(2)]
        x_of_slot = {}

        def load_x(s0, n):
            x = keep.tile([P, n, E], BF16, name="x%d" % s0, align_bytes=256)
            nc.sync.dma_start(out=x[:], in_=x_hbm[:, s0 : s0 + n, :])
            for i in range(n):
                x_of_slot[s0 + i] = x[:, i, :]

        def load_scales(j):
            for r in range(4):
                nc.sync.dma_start(
                    out=w_scales[j][r:P:32, :, :].bitcast(I32),
                    in_=scales_hbm[j][:, r:16:4, :].rearrange("g q n -> q g n").bitcast(I32),
                )

        def load_words(j):
            nc.sync.dma_start(
                out=w_words[j][:].bitcast(I32), in_=words_hbm[j].rearrange("g p n -> p g n").bitcast(I32)
            )

        def load_bias(j):
            nc.gpsimd.dma_start(out=bias_rows[0:H, j, :], in_=bias_hbm[j].rearrange("(h d) -> h d", d=D))

        def spread_bias(j, bank0):
            for half in range(2):
                spread = bank_tile(bank0 + half, [P, 4, D])
                for i in range(4):
                    h = 4 * half + i
                    nc.tensor.matmul(
                        spread[:, i, :], lhsT=pick[:, h : h + 1].to_broadcast([P, P]), rhs=bias_rows[:, j, :], start=True, stop=True
                    )
                nc.scalar.copy(
                    out=bias_all[:, j, half * BANK : (half + 1) * BANK], in_=spread[:].rearrange("p i d -> p (i d)")
                )

        def turn_bias():
            turned = bank_tile(6, [P, 2, H])
            for j in range(2):
                nc.tensor.matmul(turned[:, j, :], lhsT=bias_rows[:, j, :], rhs=pick[:], start=True, stop=True)
            nc.scalar.copy(out=bias_cols[:], in_=turned[:])

        def warm_up(n):
            idle = keep.tile([P, BANK], BF16, name="idle")
            nc.vector.memset(idle[:].bitcast(I32), 0)
            unread = bank_tile(3, [P, BANK])
            for i in range(n):
                nc.tensor.matmul(unread[:], lhsT=idle[:, 0:P], rhs=idle[:], start=True, stop=True)

        def sort_chunk(c, copy, n=T):
            ordered = work.tile([P, T, PASSES, 2, P], F32, name="ordered")
            for i in range(T - n, T):
                pairs = x_of_slot[T * c + i].bitcast(F32)
                copy(out=ordered[:, i, :, :, :], in_=pairs.rearrange("p (g r u) -> p g u r", g=PASSES, u=2))
            return ordered

        def transpose_chunk(c, order):
            grouped = work.tile([P, PASSES, T, P, 2], F32, name="grouped", align_bytes=256)
            for b, (g, a) in enumerate(order):
                turned = bank_tile(4 + b, [P, 2, 2, P])
                for i in range(2):
                    pairs = x_of_slot[T * c + a + i].bitcast(F32)
                    for u in range(2):
                        nc.tensor.transpose(turned[:, i, u, :], pairs[:, 256 * g + u : 256 * (g + 1) : 2], ident[:])
                nc.scalar.copy(out=grouped[:, g, a : a + 2, :, :], in_=turned[:].rearrange("p i u r -> p i r u"))
            return grouped

        def x_cols(c, g, i, n):
            first = ((c * PASSES + g) * T + i) * P
            return slice(first, first + n * P)

        def quantize(grouped, c, g, i, n):
            values = grouped[:].rearrange("p g i r u -> p (g i r u)")
            first = (g * T + i) * P * 2
            nc.vector.quantize_mx(
                out=x_codes[:, x_cols(c, g, i, n)].bitcast(E5M2X4),
                scales=x_scales[:, x_cols(c, g, i, n)],
                in_=values[:, first : first + n * P * 2].bitcast(BF16),
            )

        bank_count = [0]

        def next_bank(banks, shape):
            bank_count[0] += 1
            return bank_tile((bank_count[0] - 1) % banks, shape)

        def project(y, j, h0, heads, s0, slots, banks):
            width = heads * D
            per_bank = BANK // width
            n0 = h0 * D
            bias = bias_all[:, j, n0 : n0 + width].rearrange("p (h d) -> p h d", d=D)
            for b0 in range(0, slots, per_bank):
                acc = next_bank(banks, [P, per_bank, width])
                for i in range(per_bank):
                    for g in range(PASSES):
                        xc = x_cols((s0 + b0 + i) // T, g, (s0 + b0 + i) % T, 1)
                        nc.tensor.matmul_mx(
                            out=acc[:, i, :],
                            lhsT=x_codes[:, xc].bitcast(E5M2X4),
                            lhsT_scale=x_scales[:, xc],
                            rhs=w_words[j][:, g, 2 * n0 : 2 * (n0 + width)].bitcast(E2M1X4),
                            rhs_scale=w_scales[j][:, g, n0 : n0 + width],
                            start=(g == 0),
                            stop=(g == PASSES - 1),
                        )
                nc.vector.tensor_tensor(
                    out=y[:, :, b0 : b0 + per_bank, :].rearrange("p h s d -> p s h d"),
                    in0=acc[:].rearrange("p s (h d) -> p s h d", d=D),
                    in1=bias.unsqueeze(1).to_broadcast([P, per_bank, heads, D]),
                    op=ADD,
                )

        def project_turned(j, h, c):
            acc = next_bank(BANKS, [P, BANK])
            for g in range(PASSES):
                nc.tensor.matmul_mx(
                    out=acc[:],
                    lhsT=w_words[j][:, g, 2 * h * D : 2 * (h + 1) * D].bitcast(E2M1X4),
                    lhsT_scale=w_scales[j][:, g, h * D : (h + 1) * D],
                    rhs=x_codes[:, x_cols(c, g, 0, T)].bitcast(E5M2X4),
                    rhs_scale=x_scales[:, x_cols(c, g, 0, T)],
                    start=(g == 0),
                    stop=(g == PASSES - 1),
                )
            y_turned = work.tile([P, T, P], F32, name="y_turned", bufs=2)
            nc.scalar.activation(
                out=y_turned[:].rearrange("p i r -> p (i r)"),
                in_=acc[:],
                func=mybir.ActivationFunctionType.Identity,
                bias=bias_cols[:, j, h : h + 1],
            )
            return y_turned

        def turn_back(y_turned, y_cell):
            back = next_bank(BANKS, [P, T, D])
            for i in range(T):
                nc.tensor.transpose(back[:, i, :], y_turned[:, i, :], ident[:])
            nc.scalar.copy(out=y_cell, in_=back[:])

        def store(y, j, h0, heads, s0, a, b):
            nc.sync.dma_start(
                out=y_hbm[j][:, h0 : h0 + heads, (s0 + a) * D : (s0 + b) * D],
                in_=y[:, :, a:b, :].rearrange("p h s d -> p h (s d)"),
            )

        def sum_on_gpsimd(cells, sums):
            a, b = cells.shape[1], cells.shape[2]
            halves = work.tile([P, a, b, 2 * D], F32, name="halves", bufs=1)
            nc.gpsimd.tensor_tensor(out=halves[:], in0=cells[:, :, :, 0 : 2 * D], in1=cells[:, :, :, 2 * D : 4 * D], op=ADD)
            nc.gpsimd.tensor_tensor(out=sums, in0=halves[:, :, :, 0:D], in1=halves[:, :, :, D : 2 * D], op=ADD)

        def sum_on_vector(cells, sums):
            nc.vector.tensor_reduce(
                out=sums, in_=cells.rearrange("p m (t d) -> p m d t", t=T), axis=mybir.AxisListType.X, op=ADD
            )

        def finish_means(j, h0):
            part = means[j][:, h0 : h0 + 2, :, :].rearrange("p h c d -> p h (c d)")
            nc.scalar.mul(out=part, in_=part, mul=1.0 / T)
            nc.scalar.dma_start(out=mean_hbm[j][:, h0 : h0 + 2, :], in_=part)

        def wide_unit(j, h0, c, on_vector):
            y = keep.tile([P, 4, T, D], F32, name="y_wide%d_%d_%d" % (j, h0, c), align_bytes=256)
            project(y, j, h0, 4, T * c, T, 4)
            store(y, j, h0, 4, T * c, 0, T)
            cells = y[:].rearrange("p h (c t) d -> p h c (t d)", t=T)
            if on_vector:
                sum_on_vector(cells[:, 0:on_vector, 0, :], means[j][:, h0 : h0 + on_vector, c, :])
            for a in range(on_vector, 4, GSTEP):
                b = min(4, a + GSTEP)
                if b > a:
                    sum_on_gpsimd(cells[:, a:b, :, :], means[j][:, h0 + a : h0 + b, c : c + 1, :])

        def part_unit(j, h0, c0, c1, on_vector):
            n = c1 - c0
            y = keep.tile([P, 2, n * T, D], F32, name="y_part%d_%d_%d" % (j, h0, c0))
            cells = y[:].rearrange("p h (c t) d -> p h c (t d)", t=T)
            sums = means[j][:, h0 : h0 + 2, c0:c1, :]
            project(y, j, h0, 2, c0 * T, n * T, 4)
            store(y, j, h0, 2, c0 * T, 0, n * T)
            for c in range(n - on_vector, n):
                sum_on_vector(cells[:, :, c, :], sums[:, :, c, :])
            for c in range(n - on_vector):
                sum_on_gpsimd(cells[:, :, c : c + 1, :], sums[:, :, c : c + 1, :])

        def long_unit(j, h0, c0, turn, on_vector, split):
            n = CHUNKS - c0
            y = work.tile([P, 2, n * T, D], F32, name="y_long", bufs=4, align_bytes=256)
            cells = y[:].rearrange("p h (c t) d -> p h c (t d)", t=T)
            sums = means[j][:, h0 : h0 + 2, c0:CHUNKS, :]
            if turn:
                turned = [project_turned(j, h0 + i, c0) for i in range(2)]
                project(y[:, :, T : n * T, :], j, h0, 2, (c0 + 1) * T, (n - 1) * T, BANKS)
                for i in range(2):
                    turn_back(turned[i], y[:, i, 0:T, :])
                store(y, j, h0, 2, c0 * T, 0, n * T)
            elif split:
                project(y, j, h0, 2, c0 * T, (n - 1) * T, BANKS)
                store(y, j, h0, 2, c0 * T, 0, (n - 1) * T)
                project(y[:, :, (n - 1) * T : n * T, :], j, h0, 2, (CHUNKS - 1) * T, T, BANKS)
                store(y, j, h0, 2, c0 * T, (n - 1) * T, n * T)
            else:
                project(y, j, h0, 2, c0 * T, n * T, BANKS)
                store(y, j, h0, 2, c0 * T, 0, n * T)
            for c in range(n - on_vector, n):
                sum_on_vector(cells[:, :, c, :], sums[:, :, c, :])
            if n > on_vector:
                sum_on_gpsimd(cells[:, :, 0 : n - on_vector, :], sums[:, :, 0 : n - on_vector, :])

        nc.gpsimd.memset(bias_rows[:].rearrange("p j n -> p (j n)").bitcast(I32), 0)
        make_identity(nc, ident[:])
        nc.scalar.activation(out=pick[:], in_=ident[:, 0:H], func=mybir.ActivationFunctionType.Identity)

        load_bias(0)
        load_bias(1)
        load_x(0, 2)
        load_x(2, 2)
        load_scales(0)
        load_words(0)
        load_x(4, 4)
        load_scales(1)
        load_words(1)
        load_x(8, 4)
        load_x(12, 4)
        warm_up(6)
        grouped = {}
        ordered = {}
        grouped[0] = transpose_chunk(0, [(0, 0), (1, 0), (0, 2), (1, 2)])
        spread_bias(0, 4)
        for i in (0, 2):
            for g in range(PASSES):
                quantize(grouped[0], 0, g, i, 2)
        wide_unit(0, 0, 0, 0)
        spread_bias(1, 4)
        turn_bias()
        wide_unit(0, 4, 0, 0)
        grouped[1] = transpose_chunk(1, [(0, 0), (0, 2), (1, 0), (1, 2)])
        wide_unit(1, 0, 0, 0)
        quantize(grouped[1], 1, 0, 0, T)
        quantize(grouped[1], 1, 1, 0, T)
        grouped[2] = transpose_chunk(2, [(0, 0), (0, 2), (1, 0), (1, 2)])
        wide_unit(1, 4, 0, 0)
        quantize(grouped[2], 2, 0, 0, T)
        quantize(grouped[2], 2, 1, 0, T)
        grouped[3] = transpose_chunk(3, [(0, 0), (0, 2), (1, 0), (1, 2)])
        quantize(grouped[3], 3, 0, 0, T)
        quantize(grouped[3], 3, 1, 0, T)
        long_unit(0, 0, 1, 0, 0, 1)
        long_unit(0, 2, 1, 1, 1, 0)
        long_unit(0, 4, 1, 1, 1, 0)
        finish_means(0, 0)
        long_unit(0, 6, 1, 1, 1, 0)
        finish_means(0, 2)
        long_unit(1, 0, 1, 1, 1, 0)
        finish_means(0, 4)
        long_unit(1, 2, 1, 1, 1, 0)
        finish_means(0, 6)
        long_unit(1, 4, 1, 1, 2, 0)
        finish_means(1, 0)
        finish_means(1, 2)
        long_unit(1, 6, 1, 0, 2, 1)
        finish_means(1, 4)
        finish_means(1, 6)
